import numpy as np
import ml_dtypes


def mxq(x, axis, fmt="e4m3"):
    dtype, down = {"e4m3": (ml_dtypes.float8_e4m3fn, 7), "e5m2": (ml_dtypes.float8_e5m2, 14)}[fmt]
    v = np.moveaxis(np.asarray(x, np.float32).astype(ml_dtypes.bfloat16).astype(np.float64), axis, -1)
    blocks = v.reshape(v.shape[:-1] + (-1, 32))
    amax = np.abs(blocks).max(-1, keepdims=True)
    byte = np.maximum(np.where(amax > 0, np.frexp(amax)[1] - 1 + 127, 0) - down, 1)
    scale = np.exp2(byte - 127.0)
    codes = (blocks / scale).astype(np.float32).astype(dtype).astype(np.float64)
    return np.moveaxis((codes * scale).reshape(v.shape), -1, axis)


WIDE = False


def mx_kscale(k):
    if not WIDE:
        return np.ones(k)
    levels = np.array([10, -10, 5, -5, 0])
    a = np.random.permutation(np.resize(levels, k // 512 * 4)).reshape(k // 512, 4)
    idx = np.arange(k)
    return np.exp2(a[idx // 512, idx % 128 // 32])


BF16 = ml_dtypes.bfloat16


def bf(x):
    return np.asarray(x, np.float32).astype(BF16)


def f64(x):
    return np.asarray(x).astype(np.float64)


B, N, E, L, A, H1, H2, G = 256, 8, 8, 384, 128, 1024, 1024, 8


def mish(v):
    return v * np.tanh(np.log(1.0 + np.exp(v)))


def simnorm(v):
    vg = v.reshape(v.shape[:-1] + (v.shape[-1] // G, G))
    ex = np.exp(vg - vg.max(-1, keepdims=True))
    return (ex / ex.sum(-1, keepdims=True)).reshape(v.shape)


def setup_inputs():
    s = mx_kscale(H2)
    r = np.random.standard_normal
    return {"h2": bf(mish(r((B, E, H2))) * s),
            "logits": bf(r((B, N, E))),
            "W3": bf(r((E, H2, L)) * 2.0 / np.sqrt(H2) / s[:, None]),
            "b3": bf(0.3 * r((E, L)))}


def reference(h2, logits, W3, b3):
    hq = mxq(f64(h2).transpose(1, 0, 2), 2, "e4m3")
    z = (hq @ mxq(f64(W3), 1, "e4m3")) + f64(b3)[:, None, :]
    y = simnorm(z)
    lg = f64(logits)
    ex = np.exp(lg - lg.max(-1, keepdims=True))
    comb = ex / ex.sum(-1, keepdims=True)
    return sum(comb[:, :, e, None] * y[e][:, None, :] for e in range(E))

@@ -1,0 +1,272 @@
+from contextlib import ExitStack
+
+import concourse.mybir as mybir
+from concourse.masks import make_identity
+
+F32 = mybir.dt.float32
+BF16 = mybir.dt.bfloat16
+U32 = mybir.dt.uint32
+U8 = mybir.dt.uint8
+FP8X4 = mybir.dt.float8_e4m3fn_x4
+ALU = mybir.AluOpType
+ACT = mybir.ActivationFunctionType
+AX = mybir.AxisListType
+
+P = 128
+B, N, E, L, H2, G8 = 256, 8, 8, 384, 1024, 8
+BT = B // P
+NT = B // 16
+LS = 304
+NLT = (LS + P - 1) // P
+TPB = 2 if LS <= 256 else 1
+VO = LS - 2 * P
+LV = L - LS
+V_UNITS = ((0, 0), (2, 0), (4, 0), (6, 0), (7, 0))
+
+FLOPS = 2 * B * E * H2 * L + 2 * B * N * E * L
+
+
+def softmax8(nc, pool, src, dst, a, g, mul_eng, pre):
+    gmax = pool.tile([P, a, g], F32, tag=pre + "m")
+    nc.vector.tensor_reduce(out=gmax[:], in_=src, axis=AX.X, op=ALU.max)
+    ex = pool.tile([P, a, g, G8], F32, tag=pre + "e")
+    nc.vector.tensor_tensor(
+        out=ex[:], in0=src, in1=gmax[:].unsqueeze(3).to_broadcast([P, a, g, G8]), op=ALU.subtract
+    )
+    nc.scalar.activation(out=ex[:], in_=ex[:], func=ACT.Exp)
+    gsum = pool.tile([P, a, g], F32, tag=pre + "s")
+    nc.vector.tensor_reduce(out=gsum[:], in_=ex[:], axis=AX.X, op=ALU.add)
+    rec = pool.tile([P, a, g], F32, tag=pre + "r")
+    nc.vector.reciprocal(out=rec[:], in_=gsum[:])
+    mul_eng.tensor_tensor(
+        out=dst, in0=ex[:], in1=rec[:].unsqueeze(3).to_broadcast([P, a, g, G8]), op=ALU.mult
+    )
+
+
+def tile_softmoedynamics_pb_kernel(tc, h2, logits, W3, b3, out):
+    nc = tc.nc
+    with ExitStack() as ctx:
+        const = ctx.enter_context(tc.tile_pool(name="const", bufs=1))
+        raw = ctx.enter_context(tc.tile_pool(name="raw", bufs=4))
+        stage = ctx.enter_context(tc.tile_pool(name="stage", bufs=3))
+        small = ctx.enter_context(tc.tile_pool(name="small", bufs=1))
+        vwork = ctx.enter_context(tc.tile_pool(name="vwork", bufs=2))
+        pwork = ctx.enter_context(tc.tile_pool(name="pwork", bufs=3))
+        psA = ctx.enter_context(tc.psum_pool(name="psA", bufs=3))
+        psB = ctx.enter_context(tc.psum_pool(name="psB", bufs=3))
+        psC = ctx.enter_context(tc.psum_pool(name="psC", bufs=2))
+
+        out2d = out.rearrange("b n l -> (b n) l")
+
+
+        h_raw = {}
+        w_raw = {}
+
+        def load(e):
+            hr = raw.tile([P, BT * H2], BF16, tag="hr")
+            nc.sync.dma_start(
+                out=hr[:].rearrange("p (t k) -> p t k", t=BT),
+                in_=h2[:, e, :].rearrange("(t p) k -> p t k", p=P),
+            )
+            wr = raw.tile([P, 8 * L], BF16, tag="wr")
+            nc.sync.dma_start(
+                out=wr[:].rearrange("p (a r) -> p a r", a=4),
+                in_=W3[e].rearrange("(a p c) w -> p a (c w)", a=4, p=P, c=2),
+            )
+            h_raw[e] = hr
+            w_raw[e] = wr
+
+        load(0)
+        bz = const.tile([P, P], BF16)
+        nc.vector.memset(bz[:], 0.0)
+        nc.sync.dma_start(out=bz[0 : 3 * E, :], in_=b3.rearrange("e (t l) -> (e t) l", l=P))
+        lg_b = const.tile([P, BT, N * E], BF16)
+        nc.sync.dma_start(out=lg_b[:], in_=logits.rearrange("(t p) n e -> p t (n e)", p=P))
+        load(1)
+        lg_m = const.tile([P, NT, E], BF16)
+        nc.sync.dma_start(out=lg_m[:], in_=logits.rearrange("(t j) n e -> (j n) t e", j=16))
+        load(2)
+        load(3)
+
+        ident = const.tile([P, P], F32)
+        make_identity(nc, ident[:])
+        mask = const.tile([P, 16], F32)
+        nc.vector.tensor_reduce(
+            out=mask[:], in_=ident[:].rearrange("p (j n) -> p j n", n=N), axis=AX.X, op=ALU.add
+        )
+
+        bz32 = const.tile([P, P], F32)
+        nc.vector.tensor_copy(out=bz32[:], in_=bz[:])
+        pb = psC.tile([P, P], F32, tag="C")
+        nc.tensor.transpose(pb[:], bz32[:], ident[:])
+        b3T = const.tile([P, 3 * E], F32)
+        nc.vector.tensor_copy(out=b3T[:], in_=pb[:, 0 : 3 * E])
+
+        zT = const.tile([P, NLT, NT, E, 16], F32)
+        zTv = const.tile([P, E, B], F32)
+        comb_b = const.tile([P, BT, N, E], F32)
+        c_sb = const.tile([P, NT, P], F32)
+        acc = const.tile([P, BT, N, LV], F32)
+
+        codes = {}
+
+        def front(e):
+            hw = h_raw[e][:].bitcast(F32)
+            hg = stage.tile([P, 4 * 2 * B], BF16, tag="hg", align_bytes=64)
+            hgf = hg[:].bitcast(F32).rearrange("p (g b u) -> p g b u", g=2, u=2)
+            for g in range(2):
+                xt = psA.tile([P, 2, B], F32, tag="A")
+                for u in range(2):
+                    for t in range(BT):
+                        c0 = t * 512 + g * 256 + u * P
+                        nc.tensor.transpose(xt[:, u, t * P : (t + 1) * P], hw[:, c0 : c0 + P], ident[:])
+                nc.scalar.copy(out=hgf[:, g], in_=xt[:].rearrange("p u b -> p b u"))
+            wg = stage.tile([P, 8 * L], BF16, tag="wg", align_bytes=64)
+            wgv = wg[:].rearrange("p (g w t) -> p g w t", g=2, t=4)
+            wrv = w_raw[e][:].rearrange("p (g t w) -> p g t w", g=2, t=4)
+            for g in range(2):
+                dst = wgv[:, g].rearrange("p (c i) t -> p c t i", i=4)
+                src = wrv[:, g].rearrange("p t (c i) -> p c t i", i=4)
+                if (e, g) in V_UNITS:
+                    nc.vector.tensor_copy(out=dst, in_=src)
+                else:
+                    nc.scalar.copy(out=dst, in_=src)
+            hc = stage.tile([P, 2 * B], U32, tag="hc", align_bytes=64)
+            hs = stage.tile([P, 2 * B], U8, tag="hs", align_bytes=64)
+            nc.vector.quantize_mx(out=hc[:].bitcast(FP8X4), scales=hs[:], in_=hg[:])
+            wc = stage.tile([P, 2 * L], U32, tag="wc", align_bytes=64)
+            ws = stage.tile([P, 2 * L], U8, tag="ws", align_bytes=64)
+            nc.vector.quantize_mx(out=wc[:, 0:512].bitcast(FP8X4), scales=ws[:, 0:512], in_=wg[:, 0:2048])
+            nc.vector.quantize_mx(
+                out=wc[:, 512:768].bitcast(FP8X4), scales=ws[:, 512:768], in_=wg[:, 2048:3072]
+            )
+            codes[e] = (hc, hs, wc, ws)
+
+        def mx(e):
+            hc, hs, wc, ws = codes[e]
+            for t in range(3):
+                zp = psB.tile([P, B], F32, tag="B")
+                for g in range(2):
+                    c0 = g * L + t * P
+                    nc.tensor.matmul_mx(
+                        out=zp[:],
+                        lhsT=wc[:, c0 : c0 + P].bitcast(FP8X4),
+                        lhsT_scale=ws[:, c0 : c0 + P],
+                        rhs=hc[:, g * B : (g + 1) * B].bitcast(FP8X4),
+                        rhs_scale=hs[:, g * B : (g + 1) * B],
+                        start=(g == 0),
+                        stop=(g == 1),
+                    )
+                bias = b3T[:, 3 * e + t : 3 * e + t + 1]
+                if t < NLT:
+                    nc.scalar.activation(
+                        out=zT[:, t, :, e, :],
+                        in_=zp[:].rearrange("p (t j) -> p t j", j=16),
+                        func=ACT.Identity,
+                        bias=bias,
+                        scale=1.0,
+                    )
+                if t == 2:
+                    nc.scalar.activation(out=zTv[:, e, :], in_=zp[:], func=ACT.Identity, bias=bias, scale=1.0)
+
+        def vpath(q):
+            tv = psC.tile([P, 2, BT, P], F32, tag="C")
+            for i in range(2):
+                for t in range(BT):
+                    nc.tensor.transpose(tv[:, i, t, :], zTv[:, 2 * q + i, t * P : (t + 1) * P], ident[:])
+            yv = vwork.tile([P, 2 * BT, LV // G8, G8], F32, tag="yv")
+            softmax8(
+                nc,
+                vwork,
+                tv[:, :, :, VO:P].rearrange("p i t (g c) -> p (i t) g c", c=G8),
+                yv[:],
+                2 * BT,
+                LV // G8,
+                nc.vector,
+                "v",
+            )
+            for i in range(2):
+                e = 2 * q + i
+                for t in range(BT):
+                    y = yv[:, i * BT + t].rearrange("p g c -> p (g c)")
+                    for n in range(N):
+                        w = comb_b[:, t, n, e : e + 1]
+                        if e == 0:
+                            nc.vector.tensor_scalar_mul(out=acc[:, t, n, :], in0=y, scalar1=w)
+                        else:
+                            nc.vector.scalar_tensor_tensor(
+                                out=acc[:, t, n, :], in0=y, scalar=w, in1=acc[:, t, n, :], op0=ALU.mult, op1=ALU.add
+                            )
+
+        def combine_weights():
+            softmax8(
+                nc, small, lg_b[:].rearrange("p t (n e) -> p t n e", e=E), comb_b[:], BT, N, nc.vector, "a"
+            )
+            comb_m = small.tile([P, 1, NT, E], F32)
+            softmax8(nc, small, lg_m[:].unsqueeze(1), comb_m[:], 1, NT, nc.vector, "b")
+            ct = small.tile([P, NT * E, 16], F32)
+            nc.gpsimd.tensor_tensor(
+                out=ct[:],
+                in0=comb_m[:].rearrange("p o t e -> p (o t e)").unsqueeze(2).to_broadcast([P, NT * E, 16]),
+                in1=mask[:].unsqueeze(1).to_broadcast([P, NT * E, 16]),
+                op=ALU.mult,
+            )
+            ctv = ct[:].rearrange("p (t e) j -> p t (e j)", e=E)
+            for q in range(NT // 4):
+                pc = psC.tile([P, 4, P], F32, tag="C")
+                for i in range(4):
+                    nc.tensor.transpose(pc[:, i, :], ctv[:, 4 * q + i, :], ident[:])
+                nc.vector.tensor_copy(out=c_sb[:, 4 * q : 4 * q + 4, :], in_=pc[:])
+
+        def ppath(q):
+            zq = psA.tile([P, TPB, NLT * P], F32, tag="A")
+            for i in range(TPB):
+                for t in range(NLT):
+                    nc.tensor.transpose(
+                        zq[:, i, t * P : (t + 1) * P],
+                        zT[:, t, TPB * q + i].rearrange("p e j -> p (e j)"),
+                        ident[:],
+                    )
+            y = pwork.tile([P, TPB, LS // G8, G8], F32, tag="y")
+            softmax8(
+                nc,
+                pwork,
+                zq[:, :, 0:LS].rearrange("p i (g c) -> p i g c", c=G8),
+                y[:],
+                TPB,
+                LS // G8,
+                nc.gpsimd,
+                "p",
+            )
+            op = psB.tile([P, TPB, LS], F32, tag="B")
+            for i in range(TPB):
+                nc.tensor.matmul(
+                    out=op[:, i, :],
+                    lhsT=c_sb[:, TPB * q + i, :],
+                    rhs=y[:, i].rearrange("p g c -> p (g c)"),
+                    start=True,
+                    stop=True,
+                )
+            osb = pwork.tile([P, TPB, LS], F32, tag="o")
+            nc.scalar.copy(out=osb[:], in_=op[:])
+            r0 = TPB * q * P
+            nc.sync.dma_start(
+                out=out2d[r0 : r0 + TPB * P, 0:LS].rearrange("(i p) l -> p i l", p=P), in_=osb[:]
+            )
+
+        for e in range(E):
+            front(e)
+            if e + 4 < E:
+                load(e + 4)
+            if e == 1:
+                combine_weights()
+            if e >= 1:
+                mx(e - 1)
+                if (e - 1) % 2 == 1:
+                    vpath((e - 1) // 2)
+        mx(E - 1)
+        for q in range(NT // TPB):
+            ppath(q)
+        vpath(E // 2 - 1)
+        for t in range(BT):
+            nc.sync.dma_start(out=out[t * P : (t + 1) * P, :, LS:L], in_=acc[:, t])

@@ -17,50 +17,35 @@ B, N, E, L, H2, G8 = 256, 8, 8, 384, 1024, 8
 BT = B // P
 NT = B // 16
 LS = 304
-NLT = (LS + P - 1) // P
-TPB = 2 if LS <= 256 else 1
+NLT = 3
 VO = LS - 2 * P
 LV = L - LS
-V_UNITS = ((0, 0), (2, 0), (4, 0), (6, 0), (7, 0))
+GP = LS // G8
+GV = LV // G8
+V_UNITS = ((0, 0), (1, 0), (2, 0), (2, 1), (4, 0), (6, 0))
 
 FLOPS = 2 * B * E * H2 * L + 2 * B * N * E * L
 
 
-def softmax8(nc, pool, src, dst, a, g, mul_eng, pre):
-    gmax = pool.tile([P, a, g], F32, tag=pre + "m")
-    nc.vector.tensor_reduce(out=gmax[:], in_=src, axis=AX.X, op=ALU.max)
-    ex = pool.tile([P, a, g, G8], F32, tag=pre + "e")
-    nc.vector.tensor_tensor(
-        out=ex[:], in0=src, in1=gmax[:].unsqueeze(3).to_broadcast([P, a, g, G8]), op=ALU.subtract
-    )
-    nc.scalar.activation(out=ex[:], in_=ex[:], func=ACT.Exp)
-    gsum = pool.tile([P, a, g], F32, tag=pre + "s")
-    nc.vector.tensor_reduce(out=gsum[:], in_=ex[:], axis=AX.X, op=ALU.add)
-    rec = pool.tile([P, a, g], F32, tag=pre + "r")
-    nc.vector.reciprocal(out=rec[:], in_=gsum[:])
-    mul_eng.tensor_tensor(
-        out=dst, in0=ex[:], in1=rec[:].unsqueeze(3).to_broadcast([P, a, g, G8]), op=ALU.mult
-    )
+def bc(ap, a, g):
+    return ap.unsqueeze(3).to_broadcast([P, a, g, G8])
 
 
 def tile_softmoedynamics_pb_kernel(tc, h2, logits, W3, b3, out):
     nc = tc.nc
     with ExitStack() as ctx:
+        ctx.enter_context(tc.manual_schedule())
         const = ctx.enter_context(tc.tile_pool(name="const", bufs=1))
         raw = ctx.enter_context(tc.tile_pool(name="raw", bufs=4))
         stage = ctx.enter_context(tc.tile_pool(name="stage", bufs=3))
-        small = ctx.enter_context(tc.tile_pool(name="small", bufs=1))
         vwork = ctx.enter_context(tc.tile_pool(name="vwork", bufs=2))
-        pwork = ctx.enter_context(tc.tile_pool(name="pwork", bufs=3))
+        pwork = ctx.enter_context(tc.tile_pool(name="pwork", bufs=4))
         psA = ctx.enter_context(tc.psum_pool(name="psA", bufs=3))
         psB = ctx.enter_context(tc.psum_pool(name="psB", bufs=3))
         psC = ctx.enter_context(tc.psum_pool(name="psC", bufs=2))
 
         out2d = out.rearrange("b n l -> (b n) l")
-
-
-        h_raw = {}
-        w_raw = {}
+        h_raw, w_raw, xts, hgs, wgs, codes, zps, tvs, vt, pt = {}, {}, {}, {}, {}, {}, {}, {}, {}, {}
 
         def load(e):
             hr = raw.tile([P, BT * H2], BF16, tag="hr")
@@ -76,61 +61,56 @@ def tile_softmoedynamics_pb_kernel(tc, h2, logits, W3, b3, out):
             h_raw[e] = hr
             w_raw[e] = wr
 
-        load(0)
-        bz = const.tile([P, P], BF16)
-        nc.vector.memset(bz[:], 0.0)
-        nc.sync.dma_start(out=bz[0 : 3 * E, :], in_=b3.rearrange("e (t l) -> (e t) l", l=P))
-        lg_b = const.tile([P, BT, N * E], BF16)
-        nc.sync.dma_start(out=lg_b[:], in_=logits.rearrange("(t p) n e -> p t (n e)", p=P))
-        load(1)
-        lg_m = const.tile([P, NT, E], BF16)
-        nc.sync.dma_start(out=lg_m[:], in_=logits.rearrange("(t j) n e -> (j n) t e", j=16))
-        load(2)
-        load(3)
-
         ident = const.tile([P, P], F32)
-        make_identity(nc, ident[:])
         mask = const.tile([P, 16], F32)
-        nc.vector.tensor_reduce(
-            out=mask[:], in_=ident[:].rearrange("p (j n) -> p j n", n=N), axis=AX.X, op=ALU.add
-        )
-
+        bz = const.tile([P, P], BF16)
         bz32 = const.tile([P, P], F32)
-        nc.vector.tensor_copy(out=bz32[:], in_=bz[:])
-        pb = psC.tile([P, P], F32, tag="C")
-        nc.tensor.transpose(pb[:], bz32[:], ident[:])
         b3T = const.tile([P, 3 * E], F32)
-        nc.vector.tensor_copy(out=b3T[:], in_=pb[:, 0 : 3 * E])
-
+        lg_b = const.tile([P, BT, N, E], BF16)
+        lg_m = const.tile([P, 1, NT, E], BF16)
         zT = const.tile([P, NLT, NT, E, 16], F32)
         zTv = const.tile([P, E, B], F32)
         comb_b = const.tile([P, BT, N, E], F32)
+        comb_m = const.tile([P, 1, NT, E], F32)
+        ct = const.tile([P, NT * E, 16], F32)
         c_sb = const.tile([P, NT, P], F32)
         acc = const.tile([P, BT, N, LV], F32)
 
-        codes = {}
-
-        def front(e):
+        def th(e):
             hw = h_raw[e][:].bitcast(F32)
-            hg = stage.tile([P, 4 * 2 * B], BF16, tag="hg", align_bytes=64)
-            hgf = hg[:].bitcast(F32).rearrange("p (g b u) -> p g b u", g=2, u=2)
+            xts[e] = []
             for g in range(2):
                 xt = psA.tile([P, 2, B], F32, tag="A")
                 for u in range(2):
                     for t in range(BT):
                         c0 = t * 512 + g * 256 + u * P
                         nc.tensor.transpose(xt[:, u, t * P : (t + 1) * P], hw[:, c0 : c0 + P], ident[:])
-                nc.scalar.copy(out=hgf[:, g], in_=xt[:].rearrange("p u b -> p b u"))
-            wg = stage.tile([P, 8 * L], BF16, tag="wg", align_bytes=64)
-            wgv = wg[:].rearrange("p (g w t) -> p g w t", g=2, t=4)
+                xts[e].append(xt)
+
+        def ch(e):
+            hg = stage.tile([P, 4 * 2 * B], BF16, tag="hg", align_bytes=64)
+            hgf = hg[:].bitcast(F32).rearrange("p (g b u) -> p g b u", g=2, u=2)
+            for g in range(2):
+                nc.scalar.copy(out=hgf[:, g], in_=xts[e][g][:].rearrange("p u b -> p b u"))
+            hgs[e] = hg
+
+        def rg(e, on_vector):
+            if e not in wgs:
+                wg = stage.tile([P, 8 * L], BF16, tag="wg", align_bytes=64)
+                wgs[e] = wg
+            wgv = wgs[e][:].rearrange("p (g w t) -> p g w t", g=2, t=4)
             wrv = w_raw[e][:].rearrange("p (g t w) -> p g t w", g=2, t=4)
             for g in range(2):
                 dst = wgv[:, g].rearrange("p (c i) t -> p c t i", i=4)
                 src = wrv[:, g].rearrange("p t (c i) -> p c t i", i=4)
-                if (e, g) in V_UNITS:
-                    nc.vector.tensor_copy(out=dst, in_=src)
-                else:
-                    nc.scalar.copy(out=dst, in_=src)
+                if ((e, g) in V_UNITS) == on_vector:
+                    if on_vector:
+                        nc.vector.tensor_copy(out=dst, in_=src)
+                    else:
+                        nc.scalar.copy(out=dst, in_=src)
+
+        def qz(e):
+            hg, wg = hgs[e], wgs[e]
             hc = stage.tile([P, 2 * B], U32, tag="hc", align_bytes=64)
             hs = stage.tile([P, 2 * B], U8, tag="hs", align_bytes=64)
             nc.vector.quantize_mx(out=hc[:].bitcast(FP8X4), scales=hs[:], in_=hg[:])
@@ -144,6 +124,7 @@ def tile_softmoedynamics_pb_kernel(tc, h2, logits, W3, b3, out):
 
         def mx(e):
             hc, hs, wc, ws = codes[e]
+            zps[e] = []
             for t in range(3):
                 zp = psB.tile([P, B], F32, tag="B")
                 for g in range(2):
@@ -157,116 +138,203 @@ def tile_softmoedynamics_pb_kernel(tc, h2, logits, W3, b3, out):
                         start=(g == 0),
                         stop=(g == 1),
                     )
+                zps[e].append(zp)
+
+        def e1(e):
+            for t in range(3):
+                zp = zps[e][t]
                 bias = b3T[:, 3 * e + t : 3 * e + t + 1]
-                if t < NLT:
-                    nc.scalar.activation(
-                        out=zT[:, t, :, e, :],
-                        in_=zp[:].rearrange("p (t j) -> p t j", j=16),
-                        func=ACT.Identity,
-                        bias=bias,
-                        scale=1.0,
-                    )
+                nc.scalar.activation(
+                    out=zT[:, t, :, e, :],
+                    in_=zp[:].rearrange("p (t j) -> p t j", j=16),
+                    func=ACT.Identity,
+                    bias=bias,
+                    scale=1.0,
+                )
                 if t == 2:
                     nc.scalar.activation(out=zTv[:, e, :], in_=zp[:], func=ACT.Identity, bias=bias, scale=1.0)
 
-        def vpath(q):
-            tv = psC.tile([P, 2, BT, P], F32, tag="C")
-            for i in range(2):
-                for t in range(BT):
-                    nc.tensor.transpose(tv[:, i, t, :], zTv[:, 2 * q + i, t * P : (t + 1) * P], ident[:])
-            yv = vwork.tile([P, 2 * BT, LV // G8, G8], F32, tag="yv")
-            softmax8(
-                nc,
-                vwork,
-                tv[:, :, :, VO:P].rearrange("p i t (g c) -> p (i t) g c", c=G8),
-                yv[:],
-                2 * BT,
-                LV // G8,
-                nc.vector,
-                "v",
-            )
-            for i in range(2):
-                e = 2 * q + i
-                for t in range(BT):
-                    y = yv[:, i * BT + t].rearrange("p g c -> p (g c)")
-                    for n in range(N):
-                        w = comb_b[:, t, n, e : e + 1]
-                        if e == 0:
-                            nc.vector.tensor_scalar_mul(out=acc[:, t, n, :], in0=y, scalar1=w)
-                        else:
-                            nc.vector.scalar_tensor_tensor(
-                                out=acc[:, t, n, :], in0=y, scalar=w, in1=acc[:, t, n, :], op0=ALU.mult, op1=ALU.add
-                            )
+        def sm_a(pool, pre, src, a, g):
+            gmax = pool.tile([P, a, g], F32, tag=pre + "m")
+            nc.vector.tensor_reduce(out=gmax[:], in_=src, axis=AX.X, op=ALU.max)
+            ex = pool.tile([P, a, g, G8], F32, tag=pre + "e")
+            nc.vector.tensor_tensor(out=ex[:], in0=src, in1=bc(gmax[:], a, g), op=ALU.subtract)
+            return ex
 
-        def combine_weights():
-            softmax8(
-                nc, small, lg_b[:].rearrange("p t (n e) -> p t n e", e=E), comb_b[:], BT, N, nc.vector, "a"
-            )
-            comb_m = small.tile([P, 1, NT, E], F32)
-            softmax8(nc, small, lg_m[:].unsqueeze(1), comb_m[:], 1, NT, nc.vector, "b")
-            ct = small.tile([P, NT * E, 16], F32)
-            nc.gpsimd.tensor_tensor(
-                out=ct[:],
-                in0=comb_m[:].rearrange("p o t e -> p (o t e)").unsqueeze(2).to_broadcast([P, NT * E, 16]),
-                in1=mask[:].unsqueeze(1).to_broadcast([P, NT * E, 16]),
-                op=ALU.mult,
-            )
+        def sm_b(ex):
+            nc.scalar.activation(out=ex[:], in_=ex[:], func=ACT.Exp)
+
+        def sm_c(pool, pre, ex, a, g):
+            gsum = pool.tile([P, a, g], F32, tag=pre + "s")
+            nc.vector.tensor_reduce(out=gsum[:], in_=ex[:], axis=AX.X, op=ALU.add)
+            rec = pool.tile([P, a, g], F32, tag=pre + "r")
+            nc.vector.reciprocal(out=rec[:], in_=gsum[:])
+            return rec
+
+        def tv_(e):
+            tv = psC.tile([P, BT, P], F32, tag="C")
+            for t in range(BT):
+                nc.tensor.transpose(tv[:, t, :], zTv[:, e, t * P : (t + 1) * P], ident[:])
+            tvs[e] = tv
+
+        def v7(e):
+            vt[e] = sm_a(vwork, "v", tvs[e][:, :, VO:P].rearrange("p t (g c) -> p t g c", c=G8), BT, GV)
+
+        def v9(e):
+            ex = vt[e]
+            rec = sm_c(vwork, "v", ex, BT, GV)
+            nc.vector.tensor_tensor(out=ex[:], in0=ex[:], in1=bc(rec[:], BT, GV), op=ALU.mult)
+            for t in range(BT):
+                y = ex[:, t].rearrange("p g c -> p (g c)")
+                for n in range(N):
+                    w = comb_b[:, t, n, e : e + 1]
+                    if e == 0:
+                        nc.vector.tensor_scalar_mul(out=acc[:, t, n, :], in0=y, scalar1=w)
+                    else:
+                        nc.vector.scalar_tensor_tensor(
+                            out=acc[:, t, n, :], in0=y, scalar=w, in1=acc[:, t, n, :], op0=ALU.mult, op1=ALU.add
+                        )
+
+        def pc_(q, pool, tag):
             ctv = ct[:].rearrange("p (t e) j -> p t (e j)", e=E)
-            for q in range(NT // 4):
-                pc = psC.tile([P, 4, P], F32, tag="C")
-                for i in range(4):
-                    nc.tensor.transpose(pc[:, i, :], ctv[:, 4 * q + i, :], ident[:])
-                nc.vector.tensor_copy(out=c_sb[:, 4 * q : 4 * q + 4, :], in_=pc[:])
+            pc = pool.tile([P, 4, P], F32, tag=tag)
+            for i in range(4):
+                nc.tensor.transpose(pc[:, i, :], ctv[:, 4 * q + i, :], ident[:])
+            return pc
 
-        def ppath(q):
-            zq = psA.tile([P, TPB, NLT * P], F32, tag="A")
-            for i in range(TPB):
-                for t in range(NLT):
-                    nc.tensor.transpose(
-                        zq[:, i, t * P : (t + 1) * P],
-                        zT[:, t, TPB * q + i].rearrange("p e j -> p (e j)"),
-                        ident[:],
-                    )
-            y = pwork.tile([P, TPB, LS // G8, G8], F32, tag="y")
-            softmax8(
-                nc,
-                pwork,
-                zq[:, :, 0:LS].rearrange("p i (g c) -> p i g c", c=G8),
-                y[:],
-                TPB,
-                LS // G8,
-                nc.gpsimd,
-                "p",
-            )
-            op = psB.tile([P, TPB, LS], F32, tag="B")
-            for i in range(TPB):
-                nc.tensor.matmul(
-                    out=op[:, i, :],
-                    lhsT=c_sb[:, TPB * q + i, :],
-                    rhs=y[:, i].rearrange("p g c -> p (g c)"),
-                    start=True,
-                    stop=True,
+        def cc(q, pc):
+            nc.scalar.copy(out=c_sb[:, 4 * q : 4 * q + 4, :], in_=pc[:])
+
+        def t2(t):
+            zq = psA.tile([P, NLT * P], F32, tag="A")
+            for k in range(NLT):
+                nc.tensor.transpose(
+                    zq[:, k * P : (k + 1) * P], zT[:, k, t].rearrange("p e j -> p (e j)"), ident[:]
                 )
-            osb = pwork.tile([P, TPB, LS], F32, tag="o")
-            nc.scalar.copy(out=osb[:], in_=op[:])
-            r0 = TPB * q * P
-            nc.sync.dma_start(
-                out=out2d[r0 : r0 + TPB * P, 0:LS].rearrange("(i p) l -> p i l", p=P), in_=osb[:]
-            )
+            pt[t] = [zq]
 
-        for e in range(E):
-            front(e)
-            if e + 4 < E:
-                load(e + 4)
-            if e == 1:
-                combine_weights()
-            if e >= 1:
-                mx(e - 1)
-                if (e - 1) % 2 == 1:
-                    vpath((e - 1) // 2)
-        mx(E - 1)
-        for q in range(NT // TPB):
-            ppath(q)
-        vpath(E // 2 - 1)
+        def ms(t):
+            zq = pt[t][0]
+            pt[t].append(sm_a(pwork, "p", zq[:, 0:LS].rearrange("p (o g c) -> p o g c", o=1, c=G8), 1, GP))
+
+        def sr(t):
+            pt[t].append(sm_c(pwork, "p", pt[t][1], 1, GP))
+
+        def ml(t):
+            y = pwork.tile([P, 1, GP, G8], F32, tag="y")
+            nc.gpsimd.tensor_tensor(out=y[:], in0=pt[t][1][:], in1=bc(pt[t][2][:], 1, GP), op=ALU.mult)
+            pt[t].append(y)
+
+        def mm(t):
+            op = psB.tile([P, LS], F32, tag="B")
+            nc.tensor.matmul(
+                out=op[:], lhsT=c_sb[:, t, :], rhs=pt[t][3][:].rearrange("p o g c -> p (o g c)"), start=True, stop=True
+            )
+            pt[t].append(op)
+
+        def cp(t):
+            osb = pwork.tile([P, LS], F32, tag="o")
+            nc.scalar.copy(out=osb[:], in_=pt[t][4][:])
+            nc.sync.dma_start(out=out2d[t * P : (t + 1) * P, 0:LS], in_=osb[:])
+
+        load(0)
+        nc.vector.memset(bz[:], 0.0)
+        nc.sync.dma_start(out=bz[0 : 3 * E, :], in_=b3.rearrange("e (t l) -> (e t) l", l=P))
+        nc.sync.dma_start(out=lg_b[:], in_=logits.rearrange("(t p) n e -> p t n e", p=P))
+        load(1)
+        nc.sync.dma_start(out=lg_m[:, 0], in_=logits.rearrange("(t j) n e -> (j n) t e", j=16))
+        load(2)
+        load(3)
+        make_identity(nc, ident[:])
+        nc.vector.tensor_reduce(
+            out=mask[:], in_=ident[:].rearrange("p (j n) -> p j n", n=N), axis=AX.X, op=ALU.add
+        )
+        warm = const.tile([P, 1], F32)
+        nc.vector.memset(warm[:], 0.0)
+        nc.scalar.activation(out=warm[:], in_=warm[:], func=ACT.Exp)
+        nc.vector.tensor_copy(out=bz32[:], in_=bz[:])
+        th(0)
+        sa = {}
+        for i in range(E + 1):
+            if i < E:
+                ch(i)
+            if 0 <= i - 2:
+                tv_(i - 2)
+            if 0 <= i - 1:
+                mx(i - 1)
+            if i == 0:
+                pb = psC.tile([P, P], F32, tag="C")
+                nc.tensor.transpose(pb[:], bz32[:], ident[:])
+            if i + 1 < E:
+                th(i + 1)
+            if i == E:
+                pc0 = pc_(0, psA, "A")
+            if i < E:
+                rg(i, False)
+                rg(i, True)
+            if i == 0:
+                sa[0] = sm_a(vwork, "a", lg_b[:], BT, N)
+            if i == 1:
+                rec = sm_c(vwork, "a", sa[0], BT, N)
+                nc.vector.tensor_tensor(out=comb_b[:], in0=sa[0][:], in1=bc(rec[:], BT, N), op=ALU.mult)
+                sa[1] = sm_a(vwork, "b", lg_m[:], 1, NT)
+            if i == 2:
+                rec = sm_c(vwork, "b", sa[1], 1, NT)
+                nc.vector.tensor_tensor(out=comb_m[:], in0=sa[1][:], in1=bc(rec[:], 1, NT), op=ALU.mult)
+                nc.gpsimd.tensor_tensor(
+                    out=ct[:],
+                    in0=comb_m[:].rearrange("p o t e -> p (o t e)").unsqueeze(2).to_broadcast([P, NT * E, 16]),
+                    in1=mask[:].unsqueeze(1).to_broadcast([P, NT * E, 16]),
+                    op=ALU.mult,
+                )
+            if 0 <= i - 3:
+                v9(i - 3)
+            if 0 <= i - 2:
+                v7(i - 2)
+            if i < E:
+                qz(i)
+            if i == 0:
+                nc.vector.tensor_copy(out=b3T[:], in_=pb[:, 0 : 3 * E])
+            if 0 <= i - 1:
+                e1(i - 1)
+            if i == E:
+                cc(0, pc0)
+            if i < 2:
+                sm_b(sa[i])
+            if 0 <= i - 2:
+                sm_b(vt[i - 2])
+            if i + 4 < E:
+                load(i + 4)
+
+        t2(0)
+        t2(1)
+        tv_(E - 1)
+        t2(2)
+        ms(0)
+        sm_b(pt[0][1])
+        v7(E - 1)
+        sm_b(vt[E - 1])
+        pcs = {}
+        for s in range(NT + 1):
+            if s + 3 < NT:
+                t2(s + 3)
+            if s + 1 < NT:
+                ms(s + 1)
+                sm_b(pt[s + 1][1])
+            if s < NT:
+                sr(s)
+                ml(s)
+                mm(s)
+            if s in (0, 3, 6):
+                q = s // 3 + 1
+                pcs[q] = pc_(q, psC, "C")
+            if s == 1:
+                v9(E - 2)
+            if s >= 1:
+                cp(s - 1)
+            if s in (1, 4, 7):
+                q = s // 3 + 1
+                cc(q, pcs[q])
+        v9(E - 1)
         for t in range(BT):
             nc.sync.dma_start(out=out[t * P : (t + 1) * P, :, LS:L], in_=acc[:, t])

@@ -38,8 +38,8 @@ def tile_softmoedynamics_pb_kernel(tc, h2, logits, W3, b3, out):
         const = ctx.enter_context(tc.tile_pool(name="const", bufs=1))
         raw = ctx.enter_context(tc.tile_pool(name="raw", bufs=4))
         stage = ctx.enter_context(tc.tile_pool(name="stage", bufs=3))
-        vwork = ctx.enter_context(tc.tile_pool(name="vwork", bufs=2))
-        pwork = ctx.enter_context(tc.tile_pool(name="pwork", bufs=4))
+        vwork = ctx.enter_context(tc.tile_pool(name="vwork", bufs=3))
+        pwork = ctx.enter_context(tc.tile_pool(name="pwork", bufs=5))
         psA = ctx.enter_context(tc.psum_pool(name="psA", bufs=3))
         psB = ctx.enter_context(tc.psum_pool(name="psB", bufs=3))
         psC = ctx.enter_context(tc.psum_pool(name="psC", bufs=2))
@@ -109,18 +109,25 @@ def tile_softmoedynamics_pb_kernel(tc, h2, logits, W3, b3, out):
                     else:
                         nc.scalar.copy(out=dst, in_=src)
 
-        def qz(e):
-            hg, wg = hgs[e], wgs[e]
+        def qh(e):
+            hg = hgs[e]
             hc = stage.tile([P, 2 * B], U32, tag="hc", align_bytes=64)
             hs = stage.tile([P, 2 * B], U8, tag="hs", align_bytes=64)
             nc.vector.quantize_mx(out=hc[:].bitcast(FP8X4), scales=hs[:], in_=hg[:])
+            codes[e] = [hc, hs]
+
+        def qw1(e):
+            wg = wgs[e]
             wc = stage.tile([P, 2 * L], U32, tag="wc", align_bytes=64)
             ws = stage.tile([P, 2 * L], U8, tag="ws", align_bytes=64)
             nc.vector.quantize_mx(out=wc[:, 0:512].bitcast(FP8X4), scales=ws[:, 0:512], in_=wg[:, 0:2048])
+            codes[e].extend([wc, ws])
+
+        def qw2(e):
+            wg, wc, ws = wgs[e], codes[e][2], codes[e][3]
             nc.vector.quantize_mx(
                 out=wc[:, 512:768].bitcast(FP8X4), scales=ws[:, 512:768], in_=wg[:, 2048:3072]
             )
-            codes[e] = (hc, hs, wc, ws)
 
         def mx(e):
             hc, hs, wc, ws = codes[e]
@@ -154,22 +161,34 @@ def tile_softmoedynamics_pb_kernel(tc, h2, logits, W3, b3, out):
                 if t == 2:
                     nc.scalar.activation(out=zTv[:, e, :], in_=zp[:], func=ACT.Identity, bias=bias, scale=1.0)
 
-        def sm_a(pool, pre, src, a, g):
-            gmax = pool.tile([P, a, g], F32, tag=pre + "m")
-            nc.vector.tensor_reduce(out=gmax[:], in_=src, axis=AX.X, op=ALU.max)
-            ex = pool.tile([P, a, g, G8], F32, tag=pre + "e")
-            nc.vector.tensor_tensor(out=ex[:], in0=src, in1=bc(gmax[:], a, g), op=ALU.subtract)
-            return ex
+        def sm_new(pool, pre, src, a, g):
+            return {"pool": pool, "pre": pre, "src": src, "a": a, "g": g}
 
-        def sm_b(ex):
-            nc.scalar.activation(out=ex[:], in_=ex[:], func=ACT.Exp)
+        def f_max(o):
+            gmax = o["pool"].tile([P, o["a"], o["g"]], F32, tag=o["pre"] + "m")
+            nc.vector.tensor_reduce(out=gmax[:], in_=o["src"], axis=AX.X, op=ALU.max)
+            o["m"] = gmax
 
-        def sm_c(pool, pre, ex, a, g):
-            gsum = pool.tile([P, a, g], F32, tag=pre + "s")
-            nc.vector.tensor_reduce(out=gsum[:], in_=ex[:], axis=AX.X, op=ALU.add)
-            rec = pool.tile([P, a, g], F32, tag=pre + "r")
-            nc.vector.reciprocal(out=rec[:], in_=gsum[:])
-            return rec
+        def f_sub(o):
+            ex = o["pool"].tile([P, o["a"], o["g"], G8], F32, tag=o["pre"] + "e")
+            nc.vector.tensor_tensor(out=ex[:], in0=o["src"], in1=bc(o["m"][:], o["a"], o["g"]), op=ALU.subtract)
+            o["e"] = ex
+
+        def f_exp(o):
+            nc.scalar.activation(out=o["e"][:], in_=o["e"][:], func=ACT.Exp)
+
+        def f_sum(o):
+            gsum = o["pool"].tile([P, o["a"], o["g"]], F32, tag=o["pre"] + "s")
+            nc.vector.tensor_reduce(out=gsum[:], in_=o["e"][:], axis=AX.X, op=ALU.add)
+            o["s"] = gsum
+
+        def f_rec(o):
+            rec = o["pool"].tile([P, o["a"], o["g"]], F32, tag=o["pre"] + "r")
+            nc.vector.reciprocal(out=rec[:], in_=o["s"][:])
+            o["r"] = rec
+
+        def f_mul(o, eng, dst):
+            eng.tensor_tensor(out=dst, in0=o["e"][:], in1=bc(o["r"][:], o["a"], o["g"]), op=ALU.mult)
 
         def tv_(e):
             tv = psC.tile([P, BT, P], F32, tag="C")
@@ -177,23 +196,26 @@ def tile_softmoedynamics_pb_kernel(tc, h2, logits, W3, b3, out):
                 nc.tensor.transpose(tv[:, t, :], zTv[:, e, t * P : (t + 1) * P], ident[:])
             tvs[e] = tv
 
-        def v7(e):
-            vt[e] = sm_a(vwork, "v", tvs[e][:, :, VO:P].rearrange("p t (g c) -> p t g c", c=G8), BT, GV)
+        def v_new(e):
+            vt[e] = sm_new(vwork, "v", tvs[e][:, :, VO:P].rearrange("p t (g c) -> p t g c", c=G8), BT, GV)
 
-        def v9(e):
-            ex = vt[e]
-            rec = sm_c(vwork, "v", ex, BT, GV)
-            nc.vector.tensor_tensor(out=ex[:], in0=ex[:], in1=bc(rec[:], BT, GV), op=ALU.mult)
+        def v_mul(e):
+            f_mul(vt[e], nc.vector, vt[e]["e"][:])
+
+        def v_stt(e, t, n):
+            y = vt[e]["e"][:, t].rearrange("p g c -> p (g c)")
+            w = comb_b[:, t, n, e : e + 1]
+            if e == 0:
+                nc.vector.tensor_scalar_mul(out=acc[:, t, n, :], in0=y, scalar1=w)
+            else:
+                nc.vector.scalar_tensor_tensor(
+                    out=acc[:, t, n, :], in0=y, scalar=w, in1=acc[:, t, n, :], op0=ALU.mult, op1=ALU.add
+                )
+
+        def v_stt_all(e):
             for t in range(BT):
-                y = ex[:, t].rearrange("p g c -> p (g c)")
                 for n in range(N):
-                    w = comb_b[:, t, n, e : e + 1]
-                    if e == 0:
-                        nc.vector.tensor_scalar_mul(out=acc[:, t, n, :], in0=y, scalar1=w)
-                    else:
-                        nc.vector.scalar_tensor_tensor(
-                            out=acc[:, t, n, :], in0=y, scalar=w, in1=acc[:, t, n, :], op0=ALU.mult, op1=ALU.add
-                        )
+                    v_stt(e, t, n)
 
         def pc_(q, pool, tag):
             ctv = ct[:].rearrange("p (t e) j -> p t (e j)", e=E)
@@ -213,28 +235,24 @@ def tile_softmoedynamics_pb_kernel(tc, h2, logits, W3, b3, out):
                 )
             pt[t] = [zq]
 
-        def ms(t):
-            zq = pt[t][0]
-            pt[t].append(sm_a(pwork, "p", zq[:, 0:LS].rearrange("p (o g c) -> p o g c", o=1, c=G8), 1, GP))
-
-        def sr(t):
-            pt[t].append(sm_c(pwork, "p", pt[t][1], 1, GP))
+        def p_new(t):
+            pt[t].append(sm_new(pwork, "p", pt[t][0][:, 0:LS].rearrange("p (o g c) -> p o g c", o=1, c=G8), 1, GP))
 
         def ml(t):
             y = pwork.tile([P, 1, GP, G8], F32, tag="y")
-            nc.gpsimd.tensor_tensor(out=y[:], in0=pt[t][1][:], in1=bc(pt[t][2][:], 1, GP), op=ALU.mult)
+            f_mul(pt[t][1], nc.gpsimd, y[:])
             pt[t].append(y)
 
         def mm(t):
             op = psB.tile([P, LS], F32, tag="B")
             nc.tensor.matmul(
-                out=op[:], lhsT=c_sb[:, t, :], rhs=pt[t][3][:].rearrange("p o g c -> p (o g c)"), start=True, stop=True
+                out=op[:], lhsT=c_sb[:, t, :], rhs=pt[t][2][:].rearrange("p o g c -> p (o g c)"), start=True, stop=True
             )
             pt[t].append(op)
 
         def cp(t):
             osb = pwork.tile([P, LS], F32, tag="o")
-            nc.scalar.copy(out=osb[:], in_=pt[t][4][:])
+            nc.scalar.copy(out=osb[:], in_=pt[t][3][:])
             nc.sync.dma_start(out=out2d[t * P : (t + 1) * P, 0:LS], in_=osb[:])
 
         load(0)
@@ -254,33 +272,59 @@ def tile_softmoedynamics_pb_kernel(tc, h2, logits, W3, b3, out):
         nc.scalar.activation(out=warm[:], in_=warm[:], func=ACT.Exp)
         nc.vector.tensor_copy(out=bz32[:], in_=bz[:])
         th(0)
-        sa = {}
+        ch(0)
+        th(1)
+        rg(0, False)
+        sa = sm_new(vwork, "a", lg_b[:], BT, N)
+        sb = sm_new(vwork, "b", lg_m[:], 1, NT)
+
+        def chain(i, lag):
+            k = i - lag
+            if k == 0:
+                return sa
+            if k == 1:
+                return sb
+            if 2 <= k < E + 2:
+                return vt[k - 2]
+            return None
+
         for i in range(E + 1):
-            if i < E:
-                ch(i)
-            if 0 <= i - 2:
-                tv_(i - 2)
+            if i + 1 < E:
+                ch(i + 1)
+            if chain(i, 1) is not None:
+                f_exp(chain(i, 1))
+            if i + 1 < E:
+                rg(i + 1, False)
             if 0 <= i - 1:
                 mx(i - 1)
+            if 0 <= i - 2:
+                tv_(i - 2)
+                v_new(i - 2)
             if i == 0:
                 pb = psC.tile([P, P], F32, tag="C")
                 nc.tensor.transpose(pb[:], bz32[:], ident[:])
-            if i + 1 < E:
-                th(i + 1)
+            if i + 2 < E:
+                th(i + 2)
             if i == E:
                 pc0 = pc_(0, psA, "A")
+            if 0 <= i - 4:
+                v_stt_all(i - 4)
             if i < E:
-                rg(i, False)
                 rg(i, True)
-            if i == 0:
-                sa[0] = sm_a(vwork, "a", lg_b[:], BT, N)
+                qh(i)
+                qw1(i)
+            f_max(chain(i, 0))
+            if chain(i, 1) is not None:
+                f_sum(chain(i, 1))
+            f_sub(chain(i, 0))
+            if chain(i, 1) is not None:
+                f_rec(chain(i, 1))
+            if i < E:
+                qw2(i)
             if i == 1:
-                rec = sm_c(vwork, "a", sa[0], BT, N)
-                nc.vector.tensor_tensor(out=comb_b[:], in0=sa[0][:], in1=bc(rec[:], BT, N), op=ALU.mult)
-                sa[1] = sm_a(vwork, "b", lg_m[:], 1, NT)
+                f_mul(sa, nc.vector, comb_b[:])
             if i == 2:
-                rec = sm_c(vwork, "b", sa[1], 1, NT)
-                nc.vector.tensor_tensor(out=comb_m[:], in0=sa[1][:], in1=bc(rec[:], 1, NT), op=ALU.mult)
+                f_mul(sb, nc.vector, comb_m[:])
                 nc.gpsimd.tensor_tensor(
                     out=ct[:],
                     in0=comb_m[:].rearrange("p o t e -> p (o t e)").unsqueeze(2).to_broadcast([P, NT * E, 16]),
@@ -288,53 +332,79 @@ def tile_softmoedynamics_pb_kernel(tc, h2, logits, W3, b3, out):
                     op=ALU.mult,
                 )
             if 0 <= i - 3:
-                v9(i - 3)
-            if 0 <= i - 2:
-                v7(i - 2)
-            if i < E:
-                qz(i)
+                v_mul(i - 3)
             if i == 0:
                 nc.vector.tensor_copy(out=b3T[:], in_=pb[:, 0 : 3 * E])
             if 0 <= i - 1:
                 e1(i - 1)
             if i == E:
                 cc(0, pc0)
-            if i < 2:
-                sm_b(sa[i])
-            if 0 <= i - 2:
-                sm_b(vt[i - 2])
             if i + 4 < E:
                 load(i + 4)
 
+        f_exp(vt[E - 2])
         t2(0)
         t2(1)
         tv_(E - 1)
+        v_new(E - 1)
         t2(2)
-        ms(0)
-        sm_b(pt[0][1])
-        v7(E - 1)
-        sm_b(vt[E - 1])
+        fill = [("stt", E - 3, t, n) for t in range(BT) for n in range(N)]
+        fill.extend([("max", E - 1, 0, 0), ("sum", E - 2, 0, 0), ("sub", E - 1, 0, 0), ("rec", E - 2, 0, 0)])
+        fill.append(("mul", E - 2, 0, 0))
+        fill.extend([("stt", E - 2, t, n) for t in range(BT) for n in range(N)])
+        fill.extend([("sum", E - 1, 0, 0), ("rec", E - 1, 0, 0), ("mul", E - 1, 0, 0)])
+        fill.extend([("stt", E - 1, t, n) for t in range(BT) for n in range(N)])
+        pos = {"k": 0}
+
+        def filler(count):
+            for r in range(count):
+                k = pos["k"]
+                if k < len(fill):
+                    kind, e, t, n = fill[k]
+                    pos["k"] = k + 1
+                    if kind == "max":
+                        f_max(vt[e])
+                    if kind == "sub":
+                        f_sub(vt[e])
+                        f_exp(vt[e])
+                    if kind == "sum":
+                        f_sum(vt[e])
+                    if kind == "rec":
+                        f_rec(vt[e])
+                    if kind == "mul":
+                        v_mul(e)
+                    if kind == "stt":
+                        v_stt(e, t, n)
+                        if e == E - 1 and n == N - 1:
+                            nc.sync.dma_start(out=out[t * P : (t + 1) * P, :, LS:L], in_=acc[:, t])
+
         pcs = {}
-        for s in range(NT + 1):
-            if s + 3 < NT:
+        for s in range(-1, NT + 3):
+            if 0 <= s and s + 3 < NT:
                 t2(s + 3)
             if s + 1 < NT:
-                ms(s + 1)
-                sm_b(pt[s + 1][1])
-            if s < NT:
-                sr(s)
-                ml(s)
-                mm(s)
+                p_new(s + 1)
+                f_max(pt[s + 1][1])
+            if s < 15:
+                filler(1)
+            if 0 <= s - 1 < NT:
+                f_sum(pt[s - 1][1])
+            if s < 15:
+                filler(1)
+            if s + 1 < NT:
+                f_sub(pt[s + 1][1])
+                f_exp(pt[s + 1][1])
+            if 0 <= s - 1 < NT:
+                f_rec(pt[s - 1][1])
+                ml(s - 1)
+            if 0 <= s - 2 < NT:
+                mm(s - 2)
             if s in (0, 3, 6):
                 q = s // 3 + 1
                 pcs[q] = pc_(q, psC, "C")
-            if s == 1:
-                v9(E - 2)
-            if s >= 1:
-                cp(s - 1)
+            if 0 <= s - 3 < NT:
+                cp(s - 3)
             if s in (1, 4, 7):
                 q = s // 3 + 1
                 cc(q, pcs[q])
-        v9(E - 1)
-        for t in range(BT):
-            nc.sync.dma_start(out=out[t * P : (t + 1) * P, :, LS:L], in_=acc[:, t])
+        filler(len(fill))

@@ -22,7 +22,7 @@ VO = LS - 2 * P
 LV = L - LS
 GP = LS // G8
 GV = LV // G8
-V_UNITS = ((0, 0), (1, 0), (2, 0), (2, 1), (4, 0), (6, 0))
+V_UNITS = ((0, 0), (1, 0), (2, 0), (2, 1), (3, 0), (4, 0), (6, 0))
 
 FLOPS = 2 * B * E * H2 * L + 2 * B * N * E * L
 
@@ -34,7 +34,6 @@ def bc(ap, a, g):
 def tile_softmoedynamics_pb_kernel(tc, h2, logits, W3, b3, out):
     nc = tc.nc
     with ExitStack() as ctx:
-        ctx.enter_context(tc.manual_schedule())
         const = ctx.enter_context(tc.tile_pool(name="const", bufs=1))
         raw = ctx.enter_context(tc.tile_pool(name="raw", bufs=4))
         stage = ctx.enter_context(tc.tile_pool(name="stage", bufs=3))
@@ -200,7 +199,7 @@ def tile_softmoedynamics_pb_kernel(tc, h2, logits, W3, b3, out):
             vt[e] = sm_new(vwork, "v", tvs[e][:, :, VO:P].rearrange("p t (g c) -> p t g c", c=G8), BT, GV)
 
         def v_mul(e):
-            f_mul(vt[e], nc.vector, vt[e]["e"][:])
+            f_mul(vt[e], nc.gpsimd, vt[e]["e"][:])
 
         def v_stt(e, t, n):
             y = vt[e]["e"][:, t].rearrange("p g c -> p (g c)")
@@ -309,22 +308,17 @@ def tile_softmoedynamics_pb_kernel(tc, h2, logits, W3, b3, out):
                 pc0 = pc_(0, psA, "A")
             if 0 <= i - 4:
                 v_stt_all(i - 4)
+            if chain(i, 1) is not None:
+                f_sum(chain(i, 1))
             if i < E:
                 rg(i, True)
                 qh(i)
-                qw1(i)
-            f_max(chain(i, 0))
-            if chain(i, 1) is not None:
-                f_sum(chain(i, 1))
-            f_sub(chain(i, 0))
             if chain(i, 1) is not None:
                 f_rec(chain(i, 1))
-            if i < E:
-                qw2(i)
             if i == 1:
-                f_mul(sa, nc.vector, comb_b[:])
+                f_mul(sa, nc.gpsimd, comb_b[:])
             if i == 2:
-                f_mul(sb, nc.vector, comb_m[:])
+                f_mul(sb, nc.gpsimd, comb_m[:])
                 nc.gpsimd.tensor_tensor(
                     out=ct[:],
                     in0=comb_m[:].rearrange("p o t e -> p (o t e)").unsqueeze(2).to_broadcast([P, NT * E, 16]),
@@ -333,6 +327,12 @@ def tile_softmoedynamics_pb_kernel(tc, h2, logits, W3, b3, out):
                 )
             if 0 <= i - 3:
                 v_mul(i - 3)
+            if i < E:
+                qw1(i)
+            f_max(chain(i, 0))
+            if i < E:
+                qw2(i)
+            f_sub(chain(i, 0))
             if i == 0:
                 nc.vector.tensor_copy(out=b3T[:], in_=pb[:, 0 : 3 * E])
             if 0 <= i - 1:
@@ -349,10 +349,12 @@ def tile_softmoedynamics_pb_kernel(tc, h2, logits, W3, b3, out):
         v_new(E - 1)
         t2(2)
         fill = [("stt", E - 3, t, n) for t in range(BT) for n in range(N)]
-        fill.extend([("max", E - 1, 0, 0), ("sum", E - 2, 0, 0), ("sub", E - 1, 0, 0), ("rec", E - 2, 0, 0)])
-        fill.append(("mul", E - 2, 0, 0))
-        fill.extend([("stt", E - 2, t, n) for t in range(BT) for n in range(N)])
-        fill.extend([("sum", E - 1, 0, 0), ("rec", E - 1, 0, 0), ("mul", E - 1, 0, 0)])
+        fill.extend([("sum", E - 2, 0, 0), ("max", E - 1, 0, 0), ("rec", E - 2, 0, 0), ("sub", E - 1, 0, 0)])
+        fill.extend([("stt", E - 2, 0, n) for n in range(N)])
+        fill.append(("sum", E - 1, 0, 0))
+        fill.extend([("stt", E - 2, 1, n) for n in range(4)])
+        fill.append(("rec", E - 1, 0, 0))
+        fill.extend([("stt", E - 2, 1, n) for n in range(4, N)])
         fill.extend([("stt", E - 1, t, n) for t in range(BT) for n in range(N)])
         pos = {"k": 0}
 
@@ -371,7 +373,6 @@ def tile_softmoedynamics_pb_kernel(tc, h2, logits, W3, b3, out):
                         f_sum(vt[e])
                     if kind == "rec":
                         f_rec(vt[e])
-                    if kind == "mul":
                         v_mul(e)
                     if kind == "stt":
                         v_stt(e, t, n)

@@ -34,6 +34,7 @@ def bc(ap, a, g):
 def tile_softmoedynamics_pb_kernel(tc, h2, logits, W3, b3, out):
     nc = tc.nc
     with ExitStack() as ctx:
+        ctx.enter_context(tc.manual_schedule())
         const = ctx.enter_context(tc.tile_pool(name="const", bufs=1))
         raw = ctx.enter_context(tc.tile_pool(name="raw", bufs=4))
         stage = ctx.enter_context(tc.tile_pool(name="stage", bufs=3))

@@ -22,7 +22,7 @@ VO = LS - 2 * P
 LV = L - LS
 GP = LS // G8
 GV = LV // G8
-V_UNITS = ((0, 0), (1, 0), (2, 0), (2, 1), (3, 0), (4, 0), (6, 0))
+V_UNITS = ((0, 0), (1, 0), (2, 0), (2, 1), (4, 0), (6, 0))
 
 FLOPS = 2 * B * E * H2 * L + 2 * B * N * E * L
 
@@ -200,7 +200,7 @@ def tile_softmoedynamics_pb_kernel(tc, h2, logits, W3, b3, out):
             vt[e] = sm_new(vwork, "v", tvs[e][:, :, VO:P].rearrange("p t (g c) -> p t g c", c=G8), BT, GV)
 
         def v_mul(e):
-            f_mul(vt[e], nc.gpsimd, vt[e]["e"][:])
+            f_mul(vt[e], nc.vector, vt[e]["e"][:])
 
         def v_stt(e, t, n):
             y = vt[e]["e"][:, t].rearrange("p g c -> p (g c)")
@@ -240,7 +240,7 @@ def tile_softmoedynamics_pb_kernel(tc, h2, logits, W3, b3, out):
 
         def ml(t):
             y = pwork.tile([P, 1, GP, G8], F32, tag="y")
-            f_mul(pt[t][1], nc.gpsimd, y[:])
+            f_mul(pt[t][1], nc.vector if t == NT - 1 else nc.gpsimd, y[:])
             pt[t].append(y)
 
         def mm(t):
@@ -309,31 +309,35 @@ def tile_softmoedynamics_pb_kernel(tc, h2, logits, W3, b3, out):
                 pc0 = pc_(0, psA, "A")
             if 0 <= i - 4:
                 v_stt_all(i - 4)
-            if chain(i, 1) is not None:
-                f_sum(chain(i, 1))
+            if i == 3:
+                for q in range(4):
+                    nc.vector.tensor_tensor(
+                        out=ct[:, 32 * q : 32 * q + 32, :],
+                        in0=comb_m[:, 0, 4 * q : 4 * q + 4, :]
+                        .rearrange("p t e -> p (t e)")
+                        .unsqueeze(2)
+                        .to_broadcast([P, 32, 16]),
+                        in1=mask[:].unsqueeze(1).to_broadcast([P, 32, 16]),
+                        op=ALU.mult,
+                    )
             if i < E:
                 rg(i, True)
                 qh(i)
-            if chain(i, 1) is not None:
-                f_rec(chain(i, 1))
-            if i == 1:
-                f_mul(sa, nc.gpsimd, comb_b[:])
-            if i == 2:
-                f_mul(sb, nc.gpsimd, comb_m[:])
-                nc.gpsimd.tensor_tensor(
-                    out=ct[:],
-                    in0=comb_m[:].rearrange("p o t e -> p (o t e)").unsqueeze(2).to_broadcast([P, NT * E, 16]),
-                    in1=mask[:].unsqueeze(1).to_broadcast([P, NT * E, 16]),
-                    op=ALU.mult,
-                )
-            if 0 <= i - 3:
-                v_mul(i - 3)
-            if i < E:
                 qw1(i)
             f_max(chain(i, 0))
+            if chain(i, 1) is not None:
+                f_sum(chain(i, 1))
+            f_sub(chain(i, 0))
+            if chain(i, 1) is not None:
+                f_rec(chain(i, 1))
             if i < E:
                 qw2(i)
-            f_sub(chain(i, 0))
+            if i == 1:
+                f_mul(sa, nc.vector, comb_b[:])
+            if i == 2:
+                f_mul(sb, nc.vector, comb_m[:])
+            if 0 <= i - 3:
+                v_mul(i - 3)
             if i == 0:
                 nc.vector.tensor_copy(out=b3T[:], in_=pb[:, 0 : 3 * E])
             if 0 <= i - 1:
@@ -349,36 +353,12 @@ def tile_softmoedynamics_pb_kernel(tc, h2, logits, W3, b3, out):
         tv_(E - 1)
         v_new(E - 1)
         t2(2)
-        fill = [("stt", E - 3, t, n) for t in range(BT) for n in range(N)]
-        fill.extend([("sum", E - 2, 0, 0), ("max", E - 1, 0, 0), ("rec", E - 2, 0, 0), ("sub", E - 1, 0, 0)])
-        fill.extend([("stt", E - 2, 0, n) for n in range(N)])
-        fill.append(("sum", E - 1, 0, 0))
-        fill.extend([("stt", E - 2, 1, n) for n in range(4)])
-        fill.append(("rec", E - 1, 0, 0))
-        fill.extend([("stt", E - 2, 1, n) for n in range(4, N)])
-        fill.extend([("stt", E - 1, t, n) for t in range(BT) for n in range(N)])
-        pos = {"k": 0}
 
-        def filler(count):
-            for r in range(count):
-                k = pos["k"]
-                if k < len(fill):
-                    kind, e, t, n = fill[k]
-                    pos["k"] = k + 1
-                    if kind == "max":
-                        f_max(vt[e])
-                    if kind == "sub":
-                        f_sub(vt[e])
-                        f_exp(vt[e])
-                    if kind == "sum":
-                        f_sum(vt[e])
-                    if kind == "rec":
-                        f_rec(vt[e])
-                        v_mul(e)
-                    if kind == "stt":
-                        v_stt(e, t, n)
-                        if e == E - 1 and n == N - 1:
-                            nc.sync.dma_start(out=out[t * P : (t + 1) * P, :, LS:L], in_=acc[:, t])
+        def v_block(e, first, count):
+            for k in range(first, first + count):
+                v_stt(e, k // N, k % N)
+                if e == E - 1 and k % N == N - 1:
+                    nc.sync.dma_start(out=out[(k // N) * P : (k // N + 1) * P, :, LS:L], in_=acc[:, k // N])
 
         pcs = {}
         for s in range(-1, NT + 3):
@@ -387,18 +367,38 @@ def tile_softmoedynamics_pb_kernel(tc, h2, logits, W3, b3, out):
             if s + 1 < NT:
                 p_new(s + 1)
                 f_max(pt[s + 1][1])
-            if s < 15:
-                filler(1)
+            if s == -1:
+                f_max(vt[E - 1])
+            if s == 0:
+                f_sub(vt[E - 1])
+                f_exp(vt[E - 1])
+            if s == 2:
+                f_sum(vt[E - 1])
             if 0 <= s - 1 < NT:
                 f_sum(pt[s - 1][1])
-            if s < 15:
-                filler(1)
+            if s == -1:
+                f_sum(vt[E - 2])
+            if s == 0:
+                f_rec(vt[E - 2])
+            if s == 3:
+                f_rec(vt[E - 1])
             if s + 1 < NT:
                 f_sub(pt[s + 1][1])
                 f_exp(pt[s + 1][1])
             if 0 <= s - 1 < NT:
                 f_rec(pt[s - 1][1])
+            if s == NT:
+                v_block(E - 1, 0, 4)
+            if 0 <= s - 1 < NT:
                 ml(s - 1)
+            if s == 1:
+                v_block(E - 3, 0, 16)
+                v_mul(E - 2)
+            if s == 7:
+                v_block(E - 2, 0, 16)
+                v_mul(E - 1)
+            if s == NT:
+                v_block(E - 1, 4, 12)
             if 0 <= s - 2 < NT:
                 mm(s - 2)
             if s in (0, 3, 6):
@@ -409,4 +409,3 @@ def tile_softmoedynamics_pb_kernel(tc, h2, logits, W3, b3, out):
             if s in (1, 4, 7):
                 q = s // 3 + 1
                 cc(q, pcs[q])
-        filler(len(fill))

from contextlib import ExitStack

import concourse.mybir as mybir
from concourse.masks import make_identity

F32 = mybir.dt.float32
BF16 = mybir.dt.bfloat16
U32 = mybir.dt.uint32
U8 = mybir.dt.uint8
FP8X4 = mybir.dt.float8_e4m3fn_x4
ALU = mybir.AluOpType
ACT = mybir.ActivationFunctionType
AX = mybir.AxisListType

P = 128
B, N, E, L, H2, G8 = 256, 8, 8, 384, 1024, 8
BT = B // P
NT = B // 16
LS = 304
NLT = 3
VO = LS - 2 * P
LV = L - LS
GP = LS // G8
GV = LV // G8
V_UNITS = ((0, 0), (1, 0), (2, 0), (2, 1), (4, 0), (6, 0))

FLOPS = 2 * B * E * H2 * L + 2 * B * N * E * L


def bc(ap, a, g):
    return ap.unsqueeze(3).to_broadcast([P, a, g, G8])


def tile_softmoedynamics_pb_kernel(tc, h2, logits, W3, b3, out):
    nc = tc.nc
    with ExitStack() as ctx:
        ctx.enter_context(tc.manual_schedule())
        const = ctx.enter_context(tc.tile_pool(name="const", bufs=1))
        raw = ctx.enter_context(tc.tile_pool(name="raw", bufs=4))
        stage = ctx.enter_context(tc.tile_pool(name="stage", bufs=3))
        vwork = ctx.enter_context(tc.tile_pool(name="vwork", bufs=3))
        pwork = ctx.enter_context(tc.tile_pool(name="pwork", bufs=5))
        psA = ctx.enter_context(tc.psum_pool(name="psA", bufs=3))
        psB = ctx.enter_context(tc.psum_pool(name="psB", bufs=3))
        psC = ctx.enter_context(tc.psum_pool(name="psC", bufs=2))

        out2d = out.rearrange("b n l -> (b n) l")
        h_raw, w_raw, xts, hgs, wgs, codes, zps, tvs, vt, pt = {}, {}, {}, {}, {}, {}, {}, {}, {}, {}

        def load(e):
            hr = raw.tile([P, BT * H2], BF16, tag="hr")
            nc.sync.dma_start(
                out=hr[:].rearrange("p (t k) -> p t k", t=BT),
                in_=h2[:, e, :].rearrange("(t p) k -> p t k", p=P),
            )
            wr = raw.tile([P, 8 * L], BF16, tag="wr")
            nc.sync.dma_start(
                out=wr[:].rearrange("p (a r) -> p a r", a=4),
                in_=W3[e].rearrange("(a p c) w -> p a (c w)", a=4, p=P, c=2),
            )
            h_raw[e] = hr
            w_raw[e] = wr

        ident = const.tile([P, P], F32)
        mask = const.tile([P, 16], F32)
        bz = const.tile([P, P], BF16)
        bz32 = const.tile([P, P], F32)
        b3T = const.tile([P, 3 * E], F32)
        lg_b = const.tile([P, BT, N, E], BF16)
        lg_m = const.tile([P, 1, NT, E], BF16)
        zT = const.tile([P, NLT, NT, E, 16], F32)
        zTv = const.tile([P, E, B], F32)
        comb_b = const.tile([P, BT, N, E], F32)
        comb_m = const.tile([P, 1, NT, E], F32)
        ct = const.tile([P, NT * E, 16], F32)
        c_sb = const.tile([P, NT, P], F32)
        acc = const.tile([P, BT, N, LV], F32)

        def th(e):
            hw = h_raw[e][:].bitcast(F32)
            xts[e] = []
            for g in range(2):
                xt = psA.tile([P, 2, B], F32, tag="A")
                for u in range(2):
                    for t in range(BT):
                        c0 = t * 512 + g * 256 + u * P
                        nc.tensor.transpose(xt[:, u, t * P : (t + 1) * P], hw[:, c0 : c0 + P], ident[:])
                xts[e].append(xt)

        def ch(e):
            hg = stage.tile([P, 4 * 2 * B], BF16, tag="hg", align_bytes=64)
            hgf = hg[:].bitcast(F32).rearrange("p (g b u) -> p g b u", g=2, u=2)
            for g in range(2):
                nc.scalar.copy(out=hgf[:, g], in_=xts[e][g][:].rearrange("p u b -> p b u"))
            hgs[e] = hg

        def rg(e, on_vector):
            if e not in wgs:
                wg = stage.tile([P, 8 * L], BF16, tag="wg", align_bytes=64)
                wgs[e] = wg
            wgv = wgs[e][:].rearrange("p (g w t) -> p g w t", g=2, t=4)
            wrv = w_raw[e][:].rearrange("p (g t w) -> p g t w", g=2, t=4)
            for g in range(2):
                dst = wgv[:, g].rearrange("p (c i) t -> p c t i", i=4)
                src = wrv[:, g].rearrange("p t (c i) -> p c t i", i=4)
                if ((e, g) in V_UNITS) == on_vector:
                    if on_vector:
                        nc.vector.tensor_copy(out=dst, in_=src)
                    else:
                        nc.scalar.copy(out=dst, in_=src)

        def qh(e):
            hg = hgs[e]
            hc = stage.tile([P, 2 * B], U32, tag="hc", align_bytes=64)
            hs = stage.tile([P, 2 * B], U8, tag="hs", align_bytes=64)
            nc.vector.quantize_mx(out=hc[:].bitcast(FP8X4), scales=hs[:], in_=hg[:])
            codes[e] = [hc, hs]

        def qw1(e):
            wg = wgs[e]
            wc = stage.tile([P, 2 * L], U32, tag="wc", align_bytes=64)
            ws = stage.tile([P, 2 * L], U8, tag="ws", align_bytes=64)
            nc.vector.quantize_mx(out=wc[:, 0:512].bitcast(FP8X4), scales=ws[:, 0:512], in_=wg[:, 0:2048])
            codes[e].extend([wc, ws])

        def qw2(e):
            wg, wc, ws = wgs[e], codes[e][2], codes[e][3]
            nc.vector.quantize_mx(
                out=wc[:, 512:768].bitcast(FP8X4), scales=ws[:, 512:768], in_=wg[:, 2048:3072]
            )

        def mx(e):
            hc, hs, wc, ws = codes[e]
            zps[e] = []
            for t in range(3):
                zp = psB.tile([P, B], F32, tag="B")
                for g in range(2):
                    c0 = g * L + t * P
                    nc.tensor.matmul_mx(
                        out=zp[:],
                        lhsT=wc[:, c0 : c0 + P].bitcast(FP8X4),
                        lhsT_scale=ws[:, c0 : c0 + P],
                        rhs=hc[:, g * B : (g + 1) * B].bitcast(FP8X4),
                        rhs_scale=hs[:, g * B : (g + 1) * B],
                        start=(g == 0),
                        stop=(g == 1),
                    )
                zps[e].append(zp)

        def e1(e):
            for t in range(3):
                zp = zps[e][t]
                bias = b3T[:, 3 * e + t : 3 * e + t + 1]
                nc.scalar.activation(
                    out=zT[:, t, :, e, :],
                    in_=zp[:].rearrange("p (t j) -> p t j", j=16),
                    func=ACT.Identity,
                    bias=bias,
                    scale=1.0,
                )
                if t == 2:
                    nc.scalar.activation(out=zTv[:, e, :], in_=zp[:], func=ACT.Identity, bias=bias, scale=1.0)

        def sm_new(pool, pre, src, a, g):
            return {"pool": pool, "pre": pre, "src": src, "a": a, "g": g}

        def f_max(o):
            gmax = o["pool"].tile([P, o["a"], o["g"]], F32, tag=o["pre"] + "m")
            nc.vector.tensor_reduce(out=gmax[:], in_=o["src"], axis=AX.X, op=ALU.max)
            o["m"] = gmax

        def f_sub(o):
            ex = o["pool"].tile([P, o["a"], o["g"], G8], F32, tag=o["pre"] + "e")
            nc.vector.tensor_tensor(out=ex[:], in0=o["src"], in1=bc(o["m"][:], o["a"], o["g"]), op=ALU.subtract)
            o["e"] = ex

        def f_exp(o):
            nc.scalar.activation(out=o["e"][:], in_=o["e"][:], func=ACT.Exp)

        def f_sum(o):
            gsum = o["pool"].tile([P, o["a"], o["g"]], F32, tag=o["pre"] + "s")
            nc.vector.tensor_reduce(out=gsum[:], in_=o["e"][:], axis=AX.X, op=ALU.add)
            o["s"] = gsum

        def f_rec(o):
            rec = o["pool"].tile([P, o["a"], o["g"]], F32, tag=o["pre"] + "r")
            nc.vector.reciprocal(out=rec[:], in_=o["s"][:])
            o["r"] = rec

        def f_mul(o, eng, dst):
            eng.tensor_tensor(out=dst, in0=o["e"][:], in1=bc(o["r"][:], o["a"], o["g"]), op=ALU.mult)

        def tv_(e):
            tv = psC.tile([P, BT, P], F32, tag="C")
            for t in range(BT):
                nc.tensor.transpose(tv[:, t, :], zTv[:, e, t * P : (t + 1) * P], ident[:])
            tvs[e] = tv

        def v_new(e):
            vt[e] = sm_new(vwork, "v", tvs[e][:, :, VO:P].rearrange("p t (g c) -> p t g c", c=G8), BT, GV)

        def v_mul(e):
            f_mul(vt[e], nc.vector, vt[e]["e"][:])

        def v_stt(e, t, n):
            y = vt[e]["e"][:, t].rearrange("p g c -> p (g c)")
            w = comb_b[:, t, n, e : e + 1]
            if e == 0:
                nc.vector.tensor_scalar_mul(out=acc[:, t, n, :], in0=y, scalar1=w)
            else:
                nc.vector.scalar_tensor_tensor(
                    out=acc[:, t, n, :], in0=y, scalar=w, in1=acc[:, t, n, :], op0=ALU.mult, op1=ALU.add
                )

        def v_stt_all(e):
            for t in range(BT):
                for n in range(N):
                    v_stt(e, t, n)

        def pc_(q, pool, tag):
            ctv = ct[:].rearrange("p (t e) j -> p t (e j)", e=E)
            pc = pool.tile([P, 4, P], F32, tag=tag)
            for i in range(4):
                nc.tensor.transpose(pc[:, i, :], ctv[:, 4 * q + i, :], ident[:])
            return pc

        def cc(q, pc):
            nc.scalar.copy(out=c_sb[:, 4 * q : 4 * q + 4, :], in_=pc[:])

        def t2(t):
            zq = psA.tile([P, NLT * P], F32, tag="A")
            for k in range(NLT):
                nc.tensor.transpose(
                    zq[:, k * P : (k + 1) * P], zT[:, k, t].rearrange("p e j -> p (e j)"), ident[:]
                )
            pt[t] = [zq]

        def p_new(t):
            pt[t].append(sm_new(pwork, "p", pt[t][0][:, 0:LS].rearrange("p (o g c) -> p o g c", o=1, c=G8), 1, GP))

        def ml(t):
            y = pwork.tile([P, 1, GP, G8], F32, tag="y")
            f_mul(pt[t][1], nc.vector if t == NT - 1 else nc.gpsimd, y[:])
            pt[t].append(y)

        def mm(t):
            op = psB.tile([P, LS], F32, tag="B")
            nc.tensor.matmul(
                out=op[:], lhsT=c_sb[:, t, :], rhs=pt[t][2][:].rearrange("p o g c -> p (o g c)"), start=True, stop=True
            )
            pt[t].append(op)

        def cp(t):
            osb = pwork.tile([P, LS], F32, tag="o")
            nc.scalar.copy(out=osb[:], in_=pt[t][3][:])
            nc.sync.dma_start(out=out2d[t * P : (t + 1) * P, 0:LS], in_=osb[:])

        load(0)
        nc.vector.memset(bz[:], 0.0)
        nc.sync.dma_start(out=bz[0 : 3 * E, :], in_=b3.rearrange("e (t l) -> (e t) l", l=P))
        nc.sync.dma_start(out=lg_b[:], in_=logits.rearrange("(t p) n e -> p t n e", p=P))
        load(1)
        nc.sync.dma_start(out=lg_m[:, 0], in_=logits.rearrange("(t j) n e -> (j n) t e", j=16))
        load(2)
        load(3)
        make_identity(nc, ident[:])
        nc.vector.tensor_reduce(
            out=mask[:], in_=ident[:].rearrange("p (j n) -> p j n", n=N), axis=AX.X, op=ALU.add
        )
        warm = const.tile([P, 1], F32)
        nc.vector.memset(warm[:], 0.0)
        nc.scalar.activation(out=warm[:], in_=warm[:], func=ACT.Exp)
        nc.vector.tensor_copy(out=bz32[:], in_=bz[:])
        th(0)
        ch(0)
        th(1)
        rg(0, False)
        sa = sm_new(vwork, "a", lg_b[:], BT, N)
        sb = sm_new(vwork, "b", lg_m[:], 1, NT)

        def chain(i, lag):
            k = i - lag
            if k == 0:
                return sa
            if k == 1:
                return sb
            if 2 <= k < E + 2:
                return vt[k - 2]
            return None

        for i in range(E + 1):
            if i + 1 < E:
                ch(i + 1)
            if chain(i, 1) is not None:
                f_exp(chain(i, 1))
            if i + 1 < E:
                rg(i + 1, False)
            if 0 <= i - 1:
                mx(i - 1)
            if 0 <= i - 2:
                tv_(i - 2)
                v_new(i - 2)
            if i == 0:
                pb = psC.tile([P, P], F32, tag="C")
                nc.tensor.transpose(pb[:], bz32[:], ident[:])
            if i + 2 < E:
                th(i + 2)
            if i == E:
                pc0 = pc_(0, psA, "A")
            if 0 <= i - 4:
                v_stt_all(i - 4)
            if i == 3:
                for q in range(4):
                    nc.vector.tensor_tensor(
                        out=ct[:, 32 * q : 32 * q + 32, :],
                        in0=comb_m[:, 0, 4 * q : 4 * q + 4, :]
                        .rearrange("p t e -> p (t e)")
                        .unsqueeze(2)
                        .to_broadcast([P, 32, 16]),
                        in1=mask[:].unsqueeze(1).to_broadcast([P, 32, 16]),
                        op=ALU.mult,
                    )
            if i < E:
                rg(i, True)
                qh(i)
                qw1(i)
            f_max(chain(i, 0))
            if chain(i, 1) is not None:
                f_sum(chain(i, 1))
            f_sub(chain(i, 0))
            if chain(i, 1) is not None:
                f_rec(chain(i, 1))
            if i < E:
                qw2(i)
            if i == 1:
                f_mul(sa, nc.vector, comb_b[:])
            if i == 2:
                f_mul(sb, nc.vector, comb_m[:])
            if 0 <= i - 3:
                v_mul(i - 3)
            if i == 0:
                nc.vector.tensor_copy(out=b3T[:], in_=pb[:, 0 : 3 * E])
            if 0 <= i - 1:
                e1(i - 1)
            if i == E:
                cc(0, pc0)
            if i + 4 < E:
                load(i + 4)

        f_exp(vt[E - 2])
        t2(0)
        t2(1)
        tv_(E - 1)
        v_new(E - 1)
        t2(2)

        def v_block(e, first, count):
            for k in range(first, first + count):
                v_stt(e, k // N, k % N)
                if e == E - 1 and k % N == N - 1:
                    nc.sync.dma_start(out=out[(k // N) * P : (k // N + 1) * P, :, LS:L], in_=acc[:, k // N])

        pcs = {}
        for s in range(-1, NT + 3):
            if 0 <= s and s + 3 < NT:
                t2(s + 3)
            if s + 1 < NT:
                p_new(s + 1)
                f_max(pt[s + 1][1])
            if s == -1:
                f_max(vt[E - 1])
            if s == 0:
                f_sub(vt[E - 1])
                f_exp(vt[E - 1])
            if s == 2:
                f_sum(vt[E - 1])
            if 0 <= s - 1 < NT:
                f_sum(pt[s - 1][1])
            if s == -1:
                f_sum(vt[E - 2])
            if s == 0:
                f_rec(vt[E - 2])
            if s == 3:
                f_rec(vt[E - 1])
            if s + 1 < NT:
                f_sub(pt[s + 1][1])
                f_exp(pt[s + 1][1])
            if 0 <= s - 1 < NT:
                f_rec(pt[s - 1][1])
            if s == NT:
                v_block(E - 1, 0, 4)
            if 0 <= s - 1 < NT:
                ml(s - 1)
            if s == 1:
                v_block(E - 3, 0, 16)
                v_mul(E - 2)
            if s == 7:
                v_block(E - 2, 0, 16)
                v_mul(E - 1)
            if s == NT:
                v_block(E - 1, 4, 12)
            if 0 <= s - 2 < NT:
                mm(s - 2)
            if s in (0, 3, 6):
                q = s // 3 + 1
                pcs[q] = pc_(q, psC, "C")
            if 0 <= s - 3 < NT:
                cp(s - 3)
            if s in (1, 4, 7):
                q = s // 3 + 1
                cc(q, pcs[q])
